import numpy as np
import ml_dtypes

BF16 = ml_dtypes.bfloat16


def bf(x):
    return np.asarray(x, np.float32).astype(BF16)


def f32(x):
    return np.asarray(x, np.float32)


def f64(x):
    return np.asarray(x).astype(np.float64)


def striped(idx):
    return np.tile(idx.reshape(-1, 16).T, (8, 1))


C, S, T, N = 512, 2048, 512, 1024


def setup_inputs():
    return {"x": f32(np.random.standard_normal((C, S))), "anchor": f32(np.random.standard_normal((C, T))), "offs": striped(np.random.permutation(np.tile(np.arange(S), 2))[:N])}


def reference(x, anchor, offs):
    idx = offs[:16].T.reshape(-1)
    neg_anchor = -f64(anchor)
    d = f64(x)[:, idx] + np.tile(neg_anchor, (1, N // T))
    return d * d

@@ -1,0 +1,48 @@
+import concourse.mybir as mybir
+
+F32 = mybir.dt.float32
+U16 = mybir.dt.uint16
+
+P = 128
+C = 512
+S = 2048
+T = 512
+N = 1024
+BLOCKS = C // P
+HALVES = N // T
+PER_COLUMN = 16
+
+
+def tile_hybridvprloss_kernel(tc, x, anchor, offs, out):
+    nc = tc.nc
+    with (
+        tc.tile_pool(name="held", bufs=1) as held,
+        tc.tile_pool(name="blocks", bufs=BLOCKS) as blocks,
+    ):
+        offsets = held.tile([P, N // PER_COLUMN], U16, name="offsets")
+        nc.sync.dma_start(offsets[:], offs)
+
+        for b in range(BLOCKS):
+            rows = slice(b * P, (b + 1) * P)
+
+            anchor_tile = blocks.tile([P, T], F32, name="anchor_tile")
+            nc.sync.dma_start(anchor_tile[:], anchor[rows, :])
+            x_tile = blocks.tile([P, S], F32, name="x_tile")
+            nc.sync.dma_start(x_tile[:], x[rows, :])
+
+            neg_anchor = blocks.tile([P, T], F32, name="neg_anchor")
+            nc.scalar.mul(neg_anchor[:], anchor_tile[:], -1.0)
+
+            diff = blocks.tile([P, N], F32, name="diff")
+            for h in range(HALVES):
+                half_offsets = offsets[:, h * (T // PER_COLUMN) : (h + 1) * (T // PER_COLUMN)]
+                nc.vector.tensor_tensor(
+                    diff[:, h * T : (h + 1) * T],
+                    x_tile[:].indirect(half_offsets),
+                    neg_anchor[:],
+                    mybir.AluOpType.add,
+                )
+
+            squared = blocks.tile([P, N], F32, name="squared")
+            nc.scalar.activation(squared[:], diff[:], mybir.ActivationFunctionType.Square)
+            nc.sync.dma_start(out[rows, :], squared[:])

@@ -22,27 +22,33 @@ def tile_hybridvprloss_kernel(tc, x, anchor, offs, out):
         offsets = held.tile([P, N // PER_COLUMN], U16, name="offsets")
         nc.sync.dma_start(offsets[:], offs)
 
+        anchor_tiles = []
+        x_tiles = []
+        for b in range(BLOCKS):
+            rows = slice(b * P, (b + 1) * P)
+            anchor_tile = blocks.tile([P, T], F32, name="anchor_tile")
+            nc.sync.dma_start(anchor_tile[:], anchor[rows, :])
+            anchor_tiles.append(anchor_tile)
+            x_tile = blocks.tile([P, S], F32, name="x_tile")
+            nc.sync.dma_start(x_tile[:], x[rows, :])
+            x_tiles.append(x_tile)
+
         for b in range(BLOCKS):
             rows = slice(b * P, (b + 1) * P)
 
-            anchor_tile = blocks.tile([P, T], F32, name="anchor_tile")
-            nc.sync.dma_start(anchor_tile[:], anchor[rows, :])
-            x_tile = blocks.tile([P, S], F32, name="x_tile")
-            nc.sync.dma_start(x_tile[:], x[rows, :])
-
             neg_anchor = blocks.tile([P, T], F32, name="neg_anchor")
-            nc.scalar.mul(neg_anchor[:], anchor_tile[:], -1.0)
+            nc.scalar.mul(neg_anchor[:], anchor_tiles[b][:], -1.0)
 
             diff = blocks.tile([P, N], F32, name="diff")
             for h in range(HALVES):
                 half_offsets = offsets[:, h * (T // PER_COLUMN) : (h + 1) * (T // PER_COLUMN)]
                 nc.vector.tensor_tensor(
                     diff[:, h * T : (h + 1) * T],
-                    x_tile[:].indirect(half_offsets),
+                    x_tiles[b][:].indirect(half_offsets),
                     neg_anchor[:],
                     mybir.AluOpType.add,
                 )
 
             squared = blocks.tile([P, N], F32, name="squared")
             nc.scalar.activation(squared[:], diff[:], mybir.ActivationFunctionType.Square)
-            nc.sync.dma_start(out[rows, :], squared[:])
+            nc.scalar.dma_start(out[rows, :], squared[:])

@@ -18,6 +18,7 @@ def tile_hybridvprloss_kernel(tc, x, anchor, offs, out):
     with (
         tc.tile_pool(name="held", bufs=1) as held,
         tc.tile_pool(name="blocks", bufs=BLOCKS) as blocks,
+        tc.tile_pool(name="halves", bufs=BLOCKS * HALVES) as halves,
     ):
         offsets = held.tile([P, N // PER_COLUMN], U16, name="offsets")
         nc.sync.dma_start(offsets[:], offs)
@@ -39,16 +40,15 @@ def tile_hybridvprloss_kernel(tc, x, anchor, offs, out):
             neg_anchor = blocks.tile([P, T], F32, name="neg_anchor")
             nc.scalar.mul(neg_anchor[:], anchor_tiles[b][:], -1.0)
 
-            diff = blocks.tile([P, N], F32, name="diff")
             for h in range(HALVES):
                 half_offsets = offsets[:, h * (T // PER_COLUMN) : (h + 1) * (T // PER_COLUMN)]
+                diff = halves.tile([P, T], F32, name="diff")
                 nc.vector.tensor_tensor(
-                    diff[:, h * T : (h + 1) * T],
+                    diff[:],
                     x_tiles[b][:].indirect(half_offsets),
                     neg_anchor[:],
                     mybir.AluOpType.add,
                 )
-
-            squared = blocks.tile([P, N], F32, name="squared")
-            nc.scalar.activation(squared[:], diff[:], mybir.ActivationFunctionType.Square)
-            nc.scalar.dma_start(out[rows, :], squared[:])
+                squared = halves.tile([P, T], F32, name="squared")
+                nc.scalar.activation(squared[:], diff[:], mybir.ActivationFunctionType.Square)
+                nc.scalar.dma_start(out[rows, h * T : (h + 1) * T], squared[:])

@@ -51,4 +51,4 @@ def tile_hybridvprloss_kernel(tc, x, anchor, offs, out):
                 )
                 squared = halves.tile([P, T], F32, name="squared")
                 nc.scalar.activation(squared[:], diff[:], mybir.ActivationFunctionType.Square)
-                nc.scalar.dma_start(out[rows, h * T : (h + 1) * T], squared[:])
+                nc.sync.dma_start(out[rows, h * T : (h + 1) * T], squared[:])

@@ -9,7 +9,8 @@ S = 2048
 T = 512
 N = 1024
 BLOCKS = C // P
-HALVES = N // T
+PIECE = 256
+PIECES = N // PIECE
 PER_COLUMN = 16
 
 
@@ -18,7 +19,7 @@ def tile_hybridvprloss_kernel(tc, x, anchor, offs, out):
     with (
         tc.tile_pool(name="held", bufs=1) as held,
         tc.tile_pool(name="blocks", bufs=BLOCKS) as blocks,
-        tc.tile_pool(name="halves", bufs=BLOCKS * HALVES) as halves,
+        tc.tile_pool(name="pieces", bufs=BLOCKS * PIECES) as pieces,
     ):
         offsets = held.tile([P, N // PER_COLUMN], U16, name="offsets")
         nc.sync.dma_start(offsets[:], offs)
@@ -40,15 +41,16 @@ def tile_hybridvprloss_kernel(tc, x, anchor, offs, out):
             neg_anchor = blocks.tile([P, T], F32, name="neg_anchor")
             nc.scalar.mul(neg_anchor[:], anchor_tiles[b][:], -1.0)
 
-            for h in range(HALVES):
-                half_offsets = offsets[:, h * (T // PER_COLUMN) : (h + 1) * (T // PER_COLUMN)]
-                diff = halves.tile([P, T], F32, name="diff")
+            for first in range(0, N, PIECE):
+                piece_offsets = offsets[:, first // PER_COLUMN : (first + PIECE) // PER_COLUMN]
+                triplet = first % T
+                diff = pieces.tile([P, PIECE], F32, name="diff")
                 nc.vector.tensor_tensor(
                     diff[:],
-                    x_tiles[b][:].indirect(half_offsets),
-                    neg_anchor[:],
+                    x_tiles[b][:].indirect(piece_offsets),
+                    neg_anchor[:, triplet : triplet + PIECE],
                     mybir.AluOpType.add,
                 )
-                squared = halves.tile([P, T], F32, name="squared")
+                squared = pieces.tile([P, PIECE], F32, name="squared")
                 nc.scalar.activation(squared[:], diff[:], mybir.ActivationFunctionType.Square)
-                nc.sync.dma_start(out[rows, h * T : (h + 1) * T], squared[:])
+                nc.sync.dma_start(out[rows, first : first + PIECE], squared[:])

@@ -10,7 +10,6 @@ T = 512
 N = 1024
 BLOCKS = C // P
 PIECE = 256
-PIECES = N // PIECE
 PER_COLUMN = 16
 
 
@@ -19,7 +18,7 @@ def tile_hybridvprloss_kernel(tc, x, anchor, offs, out):
     with (
         tc.tile_pool(name="held", bufs=1) as held,
         tc.tile_pool(name="blocks", bufs=BLOCKS) as blocks,
-        tc.tile_pool(name="pieces", bufs=BLOCKS * PIECES) as pieces,
+        tc.tile_pool(name="pieces", bufs=N // PIECE) as pieces,
     ):
         offsets = held.tile([P, N // PER_COLUMN], U16, name="offsets")
         nc.sync.dma_start(offsets[:], offs)
@@ -41,16 +40,20 @@ def tile_hybridvprloss_kernel(tc, x, anchor, offs, out):
             neg_anchor = blocks.tile([P, T], F32, name="neg_anchor")
             nc.scalar.mul(neg_anchor[:], anchor_tiles[b][:], -1.0)
 
-            for first in range(0, N, PIECE):
-                piece_offsets = offsets[:, first // PER_COLUMN : (first + PIECE) // PER_COLUMN]
-                triplet = first % T
-                diff = pieces.tile([P, PIECE], F32, name="diff")
-                nc.vector.tensor_tensor(
-                    diff[:],
-                    x_tiles[b][:].indirect(piece_offsets),
-                    neg_anchor[:, triplet : triplet + PIECE],
-                    mybir.AluOpType.add,
-                )
-                squared = pieces.tile([P, PIECE], F32, name="squared")
+            last = b == BLOCKS - 1
+            width = PIECE if last else N
+            pool = pieces if last else blocks
+            for left in range(0, N, width):
+                diff = pool.tile([P, width], F32, name="diff")
+                for first in range(left, left + width, PIECE):
+                    piece_offsets = offsets[:, first // PER_COLUMN : (first + PIECE) // PER_COLUMN]
+                    triplet = first % T
+                    nc.vector.tensor_tensor(
+                        diff[:, first - left : first - left + PIECE],
+                        x_tiles[b][:].indirect(piece_offsets),
+                        neg_anchor[:, triplet : triplet + PIECE],
+                        mybir.AluOpType.add,
+                    )
+                squared = pool.tile([P, width], F32, name="squared")
                 nc.scalar.activation(squared[:], diff[:], mybir.ActivationFunctionType.Square)
-                nc.sync.dma_start(out[rows, first : first + PIECE], squared[:])
+                nc.sync.dma_start(out[rows, left : left + width], squared[:])

@@ -37,23 +37,21 @@ def tile_hybridvprloss_kernel(tc, x, anchor, offs, out):
         for b in range(BLOCKS):
             rows = slice(b * P, (b + 1) * P)
 
-            neg_anchor = blocks.tile([P, T], F32, name="neg_anchor")
-            nc.scalar.mul(neg_anchor[:], anchor_tiles[b][:], -1.0)
+            neg_anchor = blocks.tile([P, N], F32, name="neg_anchor")
+            for left in range(0, N, T):
+                nc.scalar.mul(neg_anchor[:, left : left + T], anchor_tiles[b][:], -1.0)
 
             last = b == BLOCKS - 1
             width = PIECE if last else N
             pool = pieces if last else blocks
-            for left in range(0, N, width):
+            for first in range(0, N, width):
                 diff = pool.tile([P, width], F32, name="diff")
-                for first in range(left, left + width, PIECE):
-                    piece_offsets = offsets[:, first // PER_COLUMN : (first + PIECE) // PER_COLUMN]
-                    triplet = first % T
-                    nc.vector.tensor_tensor(
-                        diff[:, first - left : first - left + PIECE],
-                        x_tiles[b][:].indirect(piece_offsets),
-                        neg_anchor[:, triplet : triplet + PIECE],
-                        mybir.AluOpType.add,
-                    )
+                nc.vector.tensor_tensor(
+                    diff[:],
+                    x_tiles[b][:].indirect(offsets[:, first // PER_COLUMN : (first + width) // PER_COLUMN]),
+                    neg_anchor[:, first : first + width],
+                    mybir.AluOpType.add,
+                )
                 squared = pool.tile([P, width], F32, name="squared")
                 nc.scalar.activation(squared[:], diff[:], mybir.ActivationFunctionType.Square)
-                nc.sync.dma_start(out[rows, left : left + width], squared[:])
+                nc.sync.dma_start(out[rows, first : first + width], squared[:])

@@ -9,7 +9,7 @@ S = 2048
 T = 512
 N = 1024
 BLOCKS = C // P
-PIECE = 256
+LAST_WIDTHS = (N // 2, N // 4, N // 4)
 PER_COLUMN = 16
 
 
@@ -18,7 +18,7 @@ def tile_hybridvprloss_kernel(tc, x, anchor, offs, out):
     with (
         tc.tile_pool(name="held", bufs=1) as held,
         tc.tile_pool(name="blocks", bufs=BLOCKS) as blocks,
-        tc.tile_pool(name="pieces", bufs=N // PIECE) as pieces,
+        tc.tile_pool(name="pieces", bufs=len(LAST_WIDTHS)) as pieces,
     ):
         offsets = held.tile([P, N // PER_COLUMN], U16, name="offsets")
         nc.sync.dma_start(offsets[:], offs)
@@ -42,9 +42,9 @@ def tile_hybridvprloss_kernel(tc, x, anchor, offs, out):
                 nc.scalar.mul(neg_anchor[:, left : left + T], anchor_tiles[b][:], -1.0)
 
             last = b == BLOCKS - 1
-            width = PIECE if last else N
             pool = pieces if last else blocks
-            for first in range(0, N, width):
+            first = 0
+            for width in LAST_WIDTHS if last else (N,):
                 diff = pool.tile([P, width], F32, name="diff")
                 nc.vector.tensor_tensor(
                     diff[:],
@@ -55,3 +55,4 @@ def tile_hybridvprloss_kernel(tc, x, anchor, offs, out):
                 squared = pool.tile([P, width], F32, name="squared")
                 nc.scalar.activation(squared[:], diff[:], mybir.ActivationFunctionType.Square)
                 nc.sync.dma_start(out[rows, first : first + width], squared[:])
+                first += width

@@ -53,6 +53,12 @@ def tile_hybridvprloss_kernel(tc, x, anchor, offs, out):
                     mybir.AluOpType.add,
                 )
                 squared = pool.tile([P, width], F32, name="squared")
-                nc.scalar.activation(squared[:], diff[:], mybir.ActivationFunctionType.Square)
-                nc.sync.dma_start(out[rows, first : first + width], squared[:])
+                part = width // 2 if b == BLOCKS - 2 else width
+                for left in range(0, width, part):
+                    nc.scalar.activation(
+                        squared[:, left : left + part], diff[:, left : left + part], mybir.ActivationFunctionType.Square
+                    )
+                    nc.sync.dma_start(
+                        out[rows, first + left : first + left + part], squared[:, left : left + part]
+                    )
                 first += width

@@ -9,16 +9,19 @@ S = 2048
 T = 512
 N = 1024
 BLOCKS = C // P
-LAST_WIDTHS = (N // 2, N // 4, N // 4)
+PAIR = 2
+CUT = (N // 2, N // 4, N // 4)
 PER_COLUMN = 16
 
 
 def tile_hybridvprloss_kernel(tc, x, anchor, offs, out):
     nc = tc.nc
+    x_blocks = x.rearrange("(p b) s -> p b s", b=BLOCKS)
+    anchor_blocks = anchor.rearrange("(p b) t -> p b t", b=BLOCKS)
+    out_blocks = out.rearrange("(p b) n -> p b n", b=BLOCKS)
     with (
         tc.tile_pool(name="held", bufs=1) as held,
         tc.tile_pool(name="blocks", bufs=BLOCKS) as blocks,
-        tc.tile_pool(name="pieces", bufs=len(LAST_WIDTHS)) as pieces,
     ):
         offsets = held.tile([P, N // PER_COLUMN], U16, name="offsets")
         nc.sync.dma_start(offsets[:], offs)
@@ -26,39 +29,39 @@ def tile_hybridvprloss_kernel(tc, x, anchor, offs, out):
         anchor_tiles = []
         x_tiles = []
         for b in range(BLOCKS):
-            rows = slice(b * P, (b + 1) * P)
             anchor_tile = blocks.tile([P, T], F32, name="anchor_tile")
-            nc.sync.dma_start(anchor_tile[:], anchor[rows, :])
+            nc.sync.dma_start(anchor_tile[:], anchor_blocks[:, b, :])
             anchor_tiles.append(anchor_tile)
             x_tile = blocks.tile([P, S], F32, name="x_tile")
-            nc.sync.dma_start(x_tile[:], x[rows, :])
+            nc.sync.dma_start(x_tile[:], x_blocks[:, b, :])
             x_tiles.append(x_tile)
 
+        squared = held.tile([P, BLOCKS, N], F32, name="squared")
         for b in range(BLOCKS):
-            rows = slice(b * P, (b + 1) * P)
-
             neg_anchor = blocks.tile([P, N], F32, name="neg_anchor")
             for left in range(0, N, T):
                 nc.scalar.mul(neg_anchor[:, left : left + T], anchor_tiles[b][:], -1.0)
 
-            last = b == BLOCKS - 1
-            pool = pieces if last else blocks
+            diff = blocks.tile([P, N], F32, name="diff")
             first = 0
-            for width in LAST_WIDTHS if last else (N,):
-                diff = pool.tile([P, width], F32, name="diff")
+            for width in CUT if b == BLOCKS - 1 else (N,):
                 nc.vector.tensor_tensor(
-                    diff[:],
+                    diff[:, first : first + width],
                     x_tiles[b][:].indirect(offsets[:, first // PER_COLUMN : (first + width) // PER_COLUMN]),
                     neg_anchor[:, first : first + width],
                     mybir.AluOpType.add,
                 )
-                squared = pool.tile([P, width], F32, name="squared")
-                part = width // 2 if b == BLOCKS - 2 else width
-                for left in range(0, width, part):
-                    nc.scalar.activation(
-                        squared[:, left : left + part], diff[:, left : left + part], mybir.ActivationFunctionType.Square
-                    )
-                    nc.sync.dma_start(
-                        out[rows, first + left : first + left + part], squared[:, left : left + part]
-                    )
                 first += width
+
+            first = 0
+            for width in (N,) if b < PAIR else CUT:
+                nc.scalar.activation(
+                    squared[:, b, first : first + width],
+                    diff[:, first : first + width],
+                    mybir.ActivationFunctionType.Square,
+                )
+                if b >= PAIR:
+                    nc.sync.dma_start(out_blocks[:, b, first : first + width], squared[:, b, first : first + width])
+                first += width
+            if b == PAIR - 1:
+                nc.sync.dma_start(out_blocks[:, :PAIR, :], squared[:, :PAIR, :])

@@ -2,15 +2,19 @@ import concourse.mybir as mybir
 
 F32 = mybir.dt.float32
 U16 = mybir.dt.uint16
+ADD = mybir.AluOpType.add
+SQUARE = mybir.ActivationFunctionType.Square
 
 P = 128
 C = 512
 S = 2048
 T = 512
-N = 1024
+SIDES = 2
+N = SIDES * T
 BLOCKS = C // P
+LAST = BLOCKS - 1
 PAIR = 2
-CUT = (N // 2, N // 4, N // 4)
+EARLY = 3 * T // 4
 PER_COLUMN = 16
 
 
@@ -19,49 +23,66 @@ def tile_hybridvprloss_kernel(tc, x, anchor, offs, out):
     x_blocks = x.rearrange("(p b) s -> p b s", b=BLOCKS)
     anchor_blocks = anchor.rearrange("(p b) t -> p b t", b=BLOCKS)
     out_blocks = out.rearrange("(p b) n -> p b n", b=BLOCKS)
+    last_out = out.rearrange("(p b) (side t) -> p b side t", b=BLOCKS, side=SIDES)[:, LAST]
     with (
         tc.tile_pool(name="held", bufs=1) as held,
         tc.tile_pool(name="blocks", bufs=BLOCKS) as blocks,
     ):
         offsets = held.tile([P, N // PER_COLUMN], U16, name="offsets")
-        nc.sync.dma_start(offsets[:], offs)
 
-        anchor_tiles = []
+        pair_anchors = held.tile([P, PAIR, T], F32, name="pair_anchors")
+        nc.sync.dma_start(pair_anchors[:], anchor_blocks[:, :PAIR, :])
+        nc.sync.dma_start(offsets[:], offs)
+        anchors = [pair_anchors[:, b, :] for b in range(PAIR)]
         x_tiles = []
         for b in range(BLOCKS):
-            anchor_tile = blocks.tile([P, T], F32, name="anchor_tile")
-            nc.sync.dma_start(anchor_tile[:], anchor_blocks[:, b, :])
-            anchor_tiles.append(anchor_tile)
+            if b >= PAIR:
+                early = T if b < LAST else EARLY
+                anchor_tile = held.tile([P, early], F32, name=f"anchor_tile{b}")
+                nc.sync.dma_start(anchor_tile[:], anchor_blocks[:, b, :early])
+                anchors.append(anchor_tile[:])
             x_tile = blocks.tile([P, S], F32, name="x_tile")
             nc.sync.dma_start(x_tile[:], x_blocks[:, b, :])
             x_tiles.append(x_tile)
+        late_anchors = held.tile([P, T - EARLY], F32, name="late_anchors", tag="late_anchors_then_squared")
+        nc.sync.dma_start(late_anchors[:], anchor_blocks[:, LAST, EARLY:])
 
-        squared = held.tile([P, BLOCKS, N], F32, name="squared")
-        for b in range(BLOCKS):
+        def look_up(diff, b, first, neg_anchor):
+            end = first + diff.shape[-1]
+            window = x_tiles[b][:].indirect(offsets[:, first // PER_COLUMN : end // PER_COLUMN])
+            nc.vector.tensor_tensor(diff, window, neg_anchor, ADD)
+
+        last_neg = held.tile([P, EARLY], F32, name="last_neg")
+        nc.scalar.mul(last_neg[:], anchors[LAST], -1.0)
+        last_neg_late = held.tile([P, T - EARLY], F32, name="last_neg_late")
+        nc.scalar.mul(last_neg_late[:], late_anchors[:], -1.0)
+
+        squared_pair = held.tile([P, PAIR, N], F32, name="squared_pair")
+        squared_rest = held.tile([P, BLOCKS - PAIR, N], F32, name="squared_rest", tag="late_anchors_then_squared")
+
+        for b in range(LAST):
             neg_anchor = blocks.tile([P, N], F32, name="neg_anchor")
             for left in range(0, N, T):
-                nc.scalar.mul(neg_anchor[:, left : left + T], anchor_tiles[b][:], -1.0)
-
+                nc.scalar.mul(neg_anchor[:, left : left + T], anchors[b], -1.0)
             diff = blocks.tile([P, N], F32, name="diff")
-            first = 0
-            for width in CUT if b == BLOCKS - 1 else (N,):
-                nc.vector.tensor_tensor(
-                    diff[:, first : first + width],
-                    x_tiles[b][:].indirect(offsets[:, first // PER_COLUMN : (first + width) // PER_COLUMN]),
-                    neg_anchor[:, first : first + width],
-                    mybir.AluOpType.add,
-                )
-                first += width
+            look_up(diff[:], b, 0, neg_anchor[:])
+            if b < PAIR:
+                nc.scalar.activation(squared_pair[:, b, :], diff[:], SQUARE)
+                if b == PAIR - 1:
+                    nc.sync.dma_start(out_blocks[:, :PAIR, :], squared_pair[:])
+            else:
+                for left in range(0, N, T):
+                    squared = squared_rest[:, b - PAIR, left : left + T]
+                    nc.scalar.activation(squared, diff[:, left : left + T], SQUARE)
+                    nc.sync.dma_start(out_blocks[:, b, left : left + T], squared)
 
-            first = 0
-            for width in (N,) if b < PAIR else CUT:
-                nc.scalar.activation(
-                    squared[:, b, first : first + width],
-                    diff[:, first : first + width],
-                    mybir.ActivationFunctionType.Square,
-                )
-                if b >= PAIR:
-                    nc.sync.dma_start(out_blocks[:, b, first : first + width], squared[:, b, first : first + width])
-                first += width
-            if b == PAIR - 1:
-                nc.sync.dma_start(out_blocks[:, :PAIR, :], squared[:, :PAIR, :])
+        last_diff = held.tile([P, SIDES, T], F32, name="last_diff")
+        last_squared = squared_rest[:, LAST - PAIR, :].rearrange("p (side t) -> p side t", side=SIDES)
+        for side in range(SIDES):
+            look_up(last_diff[:, side, :EARLY], LAST, side * T, last_neg[:])
+            nc.scalar.activation(last_squared[:, side, :EARLY], last_diff[:, side, :EARLY], SQUARE)
+            nc.sync.dma_start(last_out[:, side, :EARLY], last_squared[:, side, :EARLY])
+        for side in range(SIDES):
+            look_up(last_diff[:, side, EARLY:], LAST, side * T + EARLY, last_neg_late[:])
+            nc.scalar.activation(last_squared[:, side, EARLY:], last_diff[:, side, EARLY:], SQUARE)
+            nc.sync.dma_start(last_out[:, side, EARLY:], last_squared[:, side, EARLY:])

@@ -14,75 +14,73 @@ N = SIDES * T
 BLOCKS = C // P
 LAST = BLOCKS - 1
 PAIR = 2
-EARLY = 3 * T // 4
 PER_COLUMN = 16
+EARLY = 3 * T // 4
+STORES = (3 * T, 2 * T, T)
 
 
 def tile_hybridvprloss_kernel(tc, x, anchor, offs, out):
     nc = tc.nc
     x_blocks = x.rearrange("(p b) s -> p b s", b=BLOCKS)
     anchor_blocks = anchor.rearrange("(p b) t -> p b t", b=BLOCKS)
-    out_blocks = out.rearrange("(p b) n -> p b n", b=BLOCKS)
-    last_out = out.rearrange("(p b) (side t) -> p b side t", b=BLOCKS, side=SIDES)[:, LAST]
-    with (
-        tc.tile_pool(name="held", bufs=1) as held,
-        tc.tile_pool(name="blocks", bufs=BLOCKS) as blocks,
-    ):
+    out_columns = out.rearrange("(p b) n -> p (b n)", b=BLOCKS)
+    with tc.tile_pool(name="held", bufs=1) as held:
         offsets = held.tile([P, N // PER_COLUMN], U16, name="offsets")
 
         pair_anchors = held.tile([P, PAIR, T], F32, name="pair_anchors")
         nc.sync.dma_start(pair_anchors[:], anchor_blocks[:, :PAIR, :])
         nc.sync.dma_start(offsets[:], offs)
-        anchors = [pair_anchors[:, b, :] for b in range(PAIR)]
         x_tiles = []
+        anchors = []
         for b in range(BLOCKS):
             if b >= PAIR:
                 early = T if b < LAST else EARLY
-                anchor_tile = held.tile([P, early], F32, name=f"anchor_tile{b}")
+                anchor_tile = held.tile([P, early], F32, name=f"anchors{b}")
                 nc.sync.dma_start(anchor_tile[:], anchor_blocks[:, b, :early])
-                anchors.append(anchor_tile[:])
-            x_tile = blocks.tile([P, S], F32, name="x_tile")
+                anchors.append(anchor_tile)
+            x_tile = held.tile([P, S], F32, name=f"x{b}")
             nc.sync.dma_start(x_tile[:], x_blocks[:, b, :])
             x_tiles.append(x_tile)
         late_anchors = held.tile([P, T - EARLY], F32, name="late_anchors", tag="late_anchors_then_squared")
         nc.sync.dma_start(late_anchors[:], anchor_blocks[:, LAST, EARLY:])
 
-        def look_up(diff, b, first, neg_anchor):
-            end = first + diff.shape[-1]
-            window = x_tiles[b][:].indirect(offsets[:, first // PER_COLUMN : end // PER_COLUMN])
-            nc.vector.tensor_tensor(diff, window, neg_anchor, ADD)
+        neg_pair = held.tile([P, PAIR, T], F32, name="neg_pair")
+        nc.scalar.mul(neg_pair[:], pair_anchors[:], -1.0)
+        negated = [neg_pair[:, b, :] for b in range(PAIR)]
+        for b, source in enumerate(anchors + [late_anchors], start=PAIR):
+            neg = held.tile(list(source.shape), F32, name=f"neg{b}")
+            nc.scalar.mul(neg[:], source[:], -1.0)
+            negated.append(neg[:])
 
-        last_neg = held.tile([P, EARLY], F32, name="last_neg")
-        nc.scalar.mul(last_neg[:], anchors[LAST], -1.0)
-        last_neg_late = held.tile([P, T - EARLY], F32, name="last_neg_late")
-        nc.scalar.mul(last_neg_late[:], late_anchors[:], -1.0)
+        front = sum(STORES[:-1])
+        squared_front = held.tile([P, front], F32, name="squared_front")
+        squared_back = held.tile([P, BLOCKS * N - front], F32, name="squared_back", tag="late_anchors_then_squared")
+        diff = held.tile([P, BLOCKS * N], F32, name="diff")
 
-        squared_pair = held.tile([P, PAIR, N], F32, name="squared_pair")
-        squared_rest = held.tile([P, BLOCKS - PAIR, N], F32, name="squared_rest", tag="late_anchors_then_squared")
+        def squared(first, end):
+            return squared_front[:, first:end] if end <= front else squared_back[:, first - front : end - front]
 
+        def look_up(b, entry, neg):
+            first = b * N + entry
+            end = first + neg.shape[-1]
+            columns = slice(entry // PER_COLUMN, (entry + neg.shape[-1]) // PER_COLUMN)
+            nc.vector.tensor_tensor(diff[:, first:end], x_tiles[b][:].indirect(offsets[:, columns]), neg, ADD)
+            nc.scalar.activation(squared(first, end), diff[:, first:end], SQUARE)
+            return first, end
+
+        def store(first, end):
+            nc.sync.dma_start(out_columns[:, first:end], squared(first, end))
+
+        stored = 0
+        widths = list(STORES)
         for b in range(LAST):
-            neg_anchor = blocks.tile([P, N], F32, name="neg_anchor")
-            for left in range(0, N, T):
-                nc.scalar.mul(neg_anchor[:, left : left + T], anchors[b], -1.0)
-            diff = blocks.tile([P, N], F32, name="diff")
-            look_up(diff[:], b, 0, neg_anchor[:])
-            if b < PAIR:
-                nc.scalar.activation(squared_pair[:, b, :], diff[:], SQUARE)
-                if b == PAIR - 1:
-                    nc.sync.dma_start(out_blocks[:, :PAIR, :], squared_pair[:])
-            else:
-                for left in range(0, N, T):
-                    squared = squared_rest[:, b - PAIR, left : left + T]
-                    nc.scalar.activation(squared, diff[:, left : left + T], SQUARE)
-                    nc.sync.dma_start(out_blocks[:, b, left : left + T], squared)
+            for side in range(SIDES):
+                first, end = look_up(b, side * T, negated[b])
+                if end == stored + widths[0]:
+                    store(stored, end)
+                    stored = end
+                    widths.remove(widths[0])
 
-        last_diff = held.tile([P, SIDES, T], F32, name="last_diff")
-        last_squared = squared_rest[:, LAST - PAIR, :].rearrange("p (side t) -> p side t", side=SIDES)
-        for side in range(SIDES):
-            look_up(last_diff[:, side, :EARLY], LAST, side * T, last_neg[:])
-            nc.scalar.activation(last_squared[:, side, :EARLY], last_diff[:, side, :EARLY], SQUARE)
-            nc.sync.dma_start(last_out[:, side, :EARLY], last_squared[:, side, :EARLY])
-        for side in range(SIDES):
-            look_up(last_diff[:, side, EARLY:], LAST, side * T + EARLY, last_neg_late[:])
-            nc.scalar.activation(last_squared[:, side, EARLY:], last_diff[:, side, EARLY:], SQUARE)
-            nc.sync.dma_start(last_out[:, side, EARLY:], last_squared[:, side, EARLY:])
+        for start, neg in ((0, negated[LAST]), (EARLY, negated[BLOCKS])):
+            for side in range(SIDES):
+                store(*look_up(LAST, side * T + start, neg))

@@ -15,7 +15,7 @@ BLOCKS = C // P
 LAST = BLOCKS - 1
 PAIR = 2
 PER_COLUMN = 16
-EARLY = 3 * T // 4
+EARLY = 5 * T // 8
 STORES = (3 * T, 2 * T, T)
 
 

@@ -15,7 +15,7 @@ BLOCKS = C // P
 LAST = BLOCKS - 1
 PAIR = 2
 PER_COLUMN = 16
-EARLY = 5 * T // 8
+EARLY = T // 2
 STORES = (3 * T, 2 * T, T)
 
 
@@ -69,7 +69,8 @@ def tile_hybridvprloss_kernel(tc, x, anchor, offs, out):
             return first, end
 
         def store(first, end):
-            nc.sync.dma_start(out_columns[:, first:end], squared(first, end))
+            queue = nc.gpsimd if first == 0 else nc.sync
+            queue.dma_start(out_columns[:, first:end], squared(first, end))
 
         stored = 0
         widths = list(STORES)
@@ -81,6 +82,9 @@ def tile_hybridvprloss_kernel(tc, x, anchor, offs, out):
                     stored = end
                     widths.remove(widths[0])
 
-        for start, neg in ((0, negated[LAST]), (EARLY, negated[BLOCKS])):
-            for side in range(SIDES):
-                store(*look_up(LAST, side * T + start, neg))
+        for side in range(SIDES):
+            store(*look_up(LAST, side * T, negated[LAST]))
+        late = negated[BLOCKS]
+        store(*look_up(LAST, EARLY, late))
+        for part in (slice(0, EARLY // 2), slice(EARLY // 2, EARLY)):
+            store(*look_up(LAST, T + EARLY + part.start, late[:, part]))

@@ -69,8 +69,7 @@ def tile_hybridvprloss_kernel(tc, x, anchor, offs, out):
             return first, end
 
         def store(first, end):
-            queue = nc.gpsimd if first == 0 else nc.sync
-            queue.dma_start(out_columns[:, first:end], squared(first, end))
+            nc.sync.dma_start(out_columns[:, first:end], squared(first, end))
 
         stored = 0
         widths = list(STORES)
@@ -83,7 +82,12 @@ def tile_hybridvprloss_kernel(tc, x, anchor, offs, out):
                     widths.remove(widths[0])
 
         for side in range(SIDES):
-            store(*look_up(LAST, side * T, negated[LAST]))
+            look_up(LAST, side * T, negated[LAST])
+        early_halves = [
+            columns.rearrange("p (side t) -> p side t", side=SIDES)[:, :, :EARLY]
+            for columns in (out_columns[:, LAST * N :], squared(LAST * N, BLOCKS * N))
+        ]
+        nc.sync.dma_start(*early_halves)
         late = negated[BLOCKS]
         store(*look_up(LAST, EARLY, late))
         for part in (slice(0, EARLY // 2), slice(EARLY // 2, EARLY)):

@@ -28,7 +28,7 @@ def tile_hybridvprloss_kernel(tc, x, anchor, offs, out):
         offsets = held.tile([P, N // PER_COLUMN], U16, name="offsets")
 
         pair_anchors = held.tile([P, PAIR, T], F32, name="pair_anchors")
-        nc.sync.dma_start(pair_anchors[:], anchor_blocks[:, :PAIR, :])
+        nc.scalar.dma_start(pair_anchors[:], anchor_blocks[:, :PAIR, :])
         nc.sync.dma_start(offsets[:], offs)
         x_tiles = []
         anchors = []
@@ -69,7 +69,8 @@ def tile_hybridvprloss_kernel(tc, x, anchor, offs, out):
             return first, end
 
         def store(first, end):
-            nc.sync.dma_start(out_columns[:, first:end], squared(first, end))
+            queue = nc.scalar if first == STORES[0] else nc.sync
+            queue.dma_start(out_columns[:, first:end], squared(first, end))
 
         stored = 0
         widths = list(STORES)

import concourse.mybir as mybir

F32 = mybir.dt.float32
U16 = mybir.dt.uint16
ADD = mybir.AluOpType.add
SQUARE = mybir.ActivationFunctionType.Square

P = 128
C = 512
S = 2048
T = 512
SIDES = 2
N = SIDES * T
BLOCKS = C // P
LAST = BLOCKS - 1
PAIR = 2
PER_COLUMN = 16
EARLY = T // 2
STORES = (3 * T, 2 * T, T)


def tile_hybridvprloss_kernel(tc, x, anchor, offs, out):
    nc = tc.nc
    x_blocks = x.rearrange("(p b) s -> p b s", b=BLOCKS)
    anchor_blocks = anchor.rearrange("(p b) t -> p b t", b=BLOCKS)
    out_columns = out.rearrange("(p b) n -> p (b n)", b=BLOCKS)
    with tc.tile_pool(name="held", bufs=1) as held:
        offsets = held.tile([P, N // PER_COLUMN], U16, name="offsets")

        pair_anchors = held.tile([P, PAIR, T], F32, name="pair_anchors")
        nc.scalar.dma_start(pair_anchors[:], anchor_blocks[:, :PAIR, :])
        nc.sync.dma_start(offsets[:], offs)
        x_tiles = []
        anchors = []
        for b in range(BLOCKS):
            if b >= PAIR:
                early = T if b < LAST else EARLY
                anchor_tile = held.tile([P, early], F32, name=f"anchors{b}")
                nc.sync.dma_start(anchor_tile[:], anchor_blocks[:, b, :early])
                anchors.append(anchor_tile)
            x_tile = held.tile([P, S], F32, name=f"x{b}")
            nc.sync.dma_start(x_tile[:], x_blocks[:, b, :])
            x_tiles.append(x_tile)
        late_anchors = held.tile([P, T - EARLY], F32, name="late_anchors", tag="late_anchors_then_squared")
        nc.sync.dma_start(late_anchors[:], anchor_blocks[:, LAST, EARLY:])

        neg_pair = held.tile([P, PAIR, T], F32, name="neg_pair")
        nc.scalar.mul(neg_pair[:], pair_anchors[:], -1.0)
        negated = [neg_pair[:, b, :] for b in range(PAIR)]
        for b, source in enumerate(anchors + [late_anchors], start=PAIR):
            neg = held.tile(list(source.shape), F32, name=f"neg{b}")
            nc.scalar.mul(neg[:], source[:], -1.0)
            negated.append(neg[:])

        front = sum(STORES[:-1])
        squared_front = held.tile([P, front], F32, name="squared_front")
        squared_back = held.tile([P, BLOCKS * N - front], F32, name="squared_back", tag="late_anchors_then_squared")
        diff = held.tile([P, BLOCKS * N], F32, name="diff")

        def squared(first, end):
            return squared_front[:, first:end] if end <= front else squared_back[:, first - front : end - front]

        def look_up(b, entry, neg):
            first = b * N + entry
            end = first + neg.shape[-1]
            columns = slice(entry // PER_COLUMN, (entry + neg.shape[-1]) // PER_COLUMN)
            nc.vector.tensor_tensor(diff[:, first:end], x_tiles[b][:].indirect(offsets[:, columns]), neg, ADD)
            nc.scalar.activation(squared(first, end), diff[:, first:end], SQUARE)
            return first, end

        def store(first, end):
            queue = nc.scalar if first == STORES[0] else nc.sync
            queue.dma_start(out_columns[:, first:end], squared(first, end))

        stored = 0
        widths = list(STORES)
        for b in range(LAST):
            for side in range(SIDES):
                first, end = look_up(b, side * T, negated[b])
                if end == stored + widths[0]:
                    store(stored, end)
                    stored = end
                    widths.remove(widths[0])

        for side in range(SIDES):
            look_up(LAST, side * T, negated[LAST])
        early_halves = [
            columns.rearrange("p (side t) -> p side t", side=SIDES)[:, :, :EARLY]
            for columns in (out_columns[:, LAST * N :], squared(LAST * N, BLOCKS * N))
        ]
        nc.sync.dma_start(*early_halves)
        late = negated[BLOCKS]
        store(*look_up(LAST, EARLY, late))
        for part in (slice(0, EARLY // 2), slice(EARLY // 2, EARLY)):
            store(*look_up(LAST, T + EARLY + part.start, late[:, part]))
